import numpy as np
import ml_dtypes


def mxq(x, axis, fmt="e4m3"):
    dtype, down = {"e4m3": (ml_dtypes.float8_e4m3fn, 7), "e5m2": (ml_dtypes.float8_e5m2, 14)}[fmt]
    v = np.moveaxis(np.asarray(x, np.float32).astype(ml_dtypes.bfloat16).astype(np.float64), axis, -1)
    blocks = v.reshape(v.shape[:-1] + (-1, 32))
    amax = np.abs(blocks).max(-1, keepdims=True)
    byte = np.maximum(np.where(amax > 0, np.frexp(amax)[1] - 1 + 127, 0) - down, 1)
    scale = np.exp2(byte - 127.0)
    codes = (blocks / scale).astype(np.float32).astype(dtype).astype(np.float64)
    return np.moveaxis((codes * scale).reshape(v.shape), -1, axis)


WIDE = False


def mx_kscale(k):
    if not WIDE:
        return np.ones(k)
    levels = np.array([10, -10, 5, -5, 0])
    if k % 512:
        return np.exp2(np.random.permutation(np.resize(levels, k // 32))).repeat(32)
    a = np.empty((k // 512, 16))
    for p in range(k // 512):
        a[p, :8] = np.random.permutation(np.resize(levels, 8))
        for g in range(8):
            far = levels[np.abs(levels - a[p, g]) >= 10]
            a[p, g + 8] = far[np.random.randint(len(far))]
    return np.exp2(a.ravel()).repeat(32)


BF16 = ml_dtypes.bfloat16


def bf(x):
    return np.asarray(x, np.float32).astype(BF16)


def f64(x):
    return np.asarray(x).astype(np.float64)


B, T, D, H, NUM_LAYERS = 4, 2048, 512, 512, 3
EPS = 1e-8


def draw0():
    s = mx_kscale(D)
    return {"inv": bf(np.random.standard_normal((B, T, D)) * 0.5 * s),
            "Wk": bf(np.random.standard_normal((D, D)) * 2.0 / np.sqrt(D) / s[None, :]),
            "bk": bf(2.5 / np.sqrt(D) + 0.7 * np.random.standard_normal(D))}


def core(inv, Wk, bk):
    flat = f64(inv).reshape(-1, D)
    out = (mxq(flat, 1, "e4m3") @ mxq(f64(Wk), 1, "e4m3").T) + f64(bk)
    sqrtD = np.sqrt(D)
    S = out.sum(-1, keepdims=True)
    norms = np.sqrt((out * out).sum(-1, keepdims=True))
    c = out * S / (np.maximum(np.abs(out) * sqrtD, EPS) * np.maximum(norms, EPS))
    diff = np.abs(c[1:] - c[:-1]).sum(0)
    return np.broadcast_to(diff, (D, D)).copy()


def e4m3fn_bytes(y):
    return np.clip(np.asarray(y, np.float64), -448.0, 448.0).astype(np.float32).astype(ml_dtypes.float8_e4m3fn).view(np.uint8)


def e4m3fn_values(b):
    return np.asarray(b, np.uint8).view(ml_dtypes.float8_e4m3fn).astype(np.float64)


def setup_inputs():
    d = draw0()
    x0 = np.asarray(d['inv']).astype(np.float64)
    s = (np.max(np.abs(x0), axis=(0, 1), keepdims=True) / 448.0).astype(np.float32)
    out = {}
    for k, v in d.items():
        if k == 'inv':
            out['inv_bytes'] = e4m3fn_bytes(x0 / s.astype(np.float64))
            out['inv_scale'] = s
        else:
            out[k] = v
    return out


def reference(inv_bytes, inv_scale, Wk, bk):
    return core(e4m3fn_values(inv_bytes) * inv_scale.astype(np.float64), Wk, bk)

@@ -1,0 +1,308 @@
+import math
+from contextlib import ExitStack
+
+import concourse.mybir as mybir
+from concourse.masks import make_identity
+
+F32 = mybir.dt.float32
+BF16 = mybir.dt.bfloat16
+U32 = mybir.dt.uint32
+U8 = mybir.dt.uint8
+FP8 = mybir.dt.float8_e4m3fn
+FP8X4 = mybir.dt.float8_e4m3fn_x4
+ALU = mybir.AluOpType
+FUNC = mybir.ActivationFunctionType
+
+P = 128
+ROWS = 8192
+D = 512
+QUAD = 4
+QUADS = ROWS // (P * QUAD)
+BLOCKS = D // P
+EPS = 1e-8
+CLAMP = EPS / math.sqrt(D)
+
+PE_PAIRS = 3
+NEGATED = (0, 2)
+SCALAR_C = (1, 3)
+POOL_Z = (0, 1, 2)
+LATE = 13
+ORDER = (("bias", 0, 0), ("quant", 1), ("turn", 2, 0), ("guard", -1), ("bias", 0, 1), ("sum", -2, 1), ("root", -1), ("bias", 0, 2), ("square", 0, 0), ("recip", -1), ("turn", 2, 1), ("factor", -1), ("bias", 0, 3), ("sum", -2, 0), ("c", -1, 2), ("c", -1, 3), ("widen", 3), ("sum", -2, 2), ("c", -1, 1), ("c", -1, 0), ("square", 0, 1), ("mult", 1), ("square", 0, 2), ("square", 0, 3), ("wq", -3), ("pairs", -1), ("clamp", 0), ("sum", -2, 3))
+
+FLOPS = 2 * ROWS * D * D
+
+
+def tile_dispatcher_pa_kernel(tc, inv_bytes, inv_scale, Wk, bk, out):
+    nc = tc.nc
+
+    with ExitStack() as ctx:
+        const = ctx.enter_context(tc.tile_pool(name="const", bufs=1))
+        raw = ctx.enter_context(tc.tile_pool(name="raw", bufs=1))
+        work = ctx.enter_context(tc.tile_pool(name="work", bufs=2))
+        small = ctx.enter_context(tc.tile_pool(name="small", bufs=4))
+        psum = ctx.enter_context(tc.psum_pool(name="psum", bufs=2))
+        ctx.enter_context(tc.manual_schedule())
+
+        scale_rep = const.tile([P, QUAD, D], F32, name="scale_rep")
+        nc.sync.dma_start(
+            out=scale_rep[:, 0, :],
+            in_=inv_scale.rearrange("a b k -> (a b k)").partition_broadcast(P),
+        )
+        w_rows = const.tile([P, BLOCKS * D], BF16, name="w_rows")
+        nc.scalar.dma_start(
+            out=w_rows[:].rearrange("n (a k) -> n a k", a=BLOCKS),
+            in_=Wk.rearrange("(a n) k -> n a k", n=P),
+        )
+        bias_rep = const.tile([P, D], BF16, name="bias_rep")
+        nc.scalar.dma_start(out=bias_rep[:], in_=bk.partition_broadcast(P))
+
+        bytes_view = inv_bytes.rearrange("b t k -> (b t) k").rearrange(
+            "(p j) k -> p (j k)", p=P
+        )
+        byte_tiles = {}
+        for q in range(QUADS):
+            byte_tiles[q] = raw.tile([P, QUAD * D], U8, name="inv_bytes_%d" % q)
+            nc.sync.dma_start(
+                out=byte_tiles[q][:],
+                in_=bytes_view[:, q * QUAD * D : (q + 1) * QUAD * D],
+            )
+
+        one = const.tile([P, 1], F32, name="one")
+        nc.vector.memset(one[:], 1.0)
+        warm = const.tile([P, 1], F32, name="warm")
+        nc.scalar.activation(out=warm[:], in_=one[:], func=FUNC.Sqrt)
+
+        ident = const.tile([P, P], F32, name="ident")
+        make_identity(nc, ident[:])
+        shift = const.tile([P, P], F32, name="shift")
+        nc.vector.memset(shift[:], 0.0)
+        nc.vector.tensor_copy(out=shift[:, 0 : P - 1], in_=ident[:, 1:P])
+        nc.vector.tensor_copy(out=scale_rep[:, 1, :], in_=scale_rep[:, 0, :])
+        nc.vector.tensor_copy(out=scale_rep[:, 2:4, :], in_=scale_rep[:, 0:2, :])
+
+        sums = const.tile([P, BLOCKS, QUADS + 1], F32, name="sums")
+
+        wide, grouped, codes, planes = {}, {}, {}, {}
+        banks, outs, clamped, cs, dv = {}, {}, {}, {}, {}
+        row_sum, row_sq, scaled_sq, root, inv_root, factor = {}, {}, {}, {}, {}, {}
+
+        def turn_half(src, dst, h):
+            sw = src[:].bitcast(F32).rearrange("p (a m u) -> p a m u", a=QUAD, u=2)
+            dw = dst[:].bitcast(F32).rearrange("p (a r u) -> p a r u", a=QUAD, u=2)
+            xt = psum.tile([P, 2, 2, P], F32, name="xt", tag="xt", bufs=2)
+            for a in range(2):
+                for u in range(2):
+                    nc.tensor.transpose(
+                        out=xt[:, a, u, :], in_=sw[:, 2 * h + a, :, u], identity=ident[:]
+                    )
+            nc.scalar.copy(
+                out=dw[:, 2 * h : 2 * h + 2, :, :],
+                in_=xt[:].rearrange("p a u r -> p a r u"),
+            )
+
+        def st_widen(q):
+            wide[q] = work.tile([P, QUAD * D], BF16, name="wide", tag="wide", align_bytes=64)
+            nc.vector.tensor_tensor(
+                out=wide[q][:],
+                in0=byte_tiles[q][:].bitcast(FP8),
+                in1=scale_rep[:].rearrange("p a k -> p (a k)"),
+                op=ALU.mult,
+            )
+
+        def st_turn(q, h):
+            if h == 0:
+                grouped[q] = work.tile([P, QUAD * D], BF16, name="grouped", tag="grouped", align_bytes=64)
+            turn_half(wide[q], grouped[q], h)
+
+        def st_quantize(q):
+            codes[q] = work.tile([P, QUAD * P], U32, name="x_codes", tag="x_codes", align_bytes=64)
+            planes[q] = work.tile([P, QUAD * P], U8, name="x_planes", tag="x_planes", align_bytes=64)
+            nc.vector.quantize_mx(
+                out=codes[q][:].bitcast(FP8X4), scales=planes[q][:], in_=grouped[q][:]
+            )
+
+        def st_multiply(q):
+            for a in range(QUAD):
+                banks[(q, a)] = psum.tile([P, D], F32, name="mx", tag="mx", bufs=4)
+                nc.tensor.matmul_mx(
+                    out=banks[(q, a)][:],
+                    lhsT=codes[q][:, a * P : (a + 1) * P].bitcast(FP8X4),
+                    lhsT_scale=planes[q][:, a * P : (a + 1) * P],
+                    rhs=w_codes[:].bitcast(FP8X4),
+                    rhs_scale=w_planes[:],
+                    start=True,
+                    stop=True,
+                )
+
+        def st_bias(q, a):
+            if a == 0:
+                outs[q] = work.tile([P, QUAD, D], F32, name="outs", tag="outs")
+                row_sum[q] = small.tile([P, QUAD], F32, name="row_sum", tag="row_sum")
+                clamped[q] = work.tile([P, QUAD, D], F32, name="clamped", tag="clamped")
+            nc.vector.scalar_tensor_tensor(
+                out=outs[q][:, a, :], in0=banks[(q, a)][:], scalar=1.0, in1=bias_rep[:],
+                op0=ALU.mult, op1=ALU.add, accum_out=row_sum[q][:, a : a + 1],
+            )
+            if a in POOL_Z:
+                nc.gpsimd.tensor_scalar(
+                    out=clamped[q][:, a, :], in0=outs[q][:, a, :], scalar1=CLAMP, scalar2=-CLAMP,
+                    op0=ALU.min, op1=ALU.max,
+                )
+
+        def st_square(q, a):
+            if a == 0:
+                row_sq[q] = small.tile([P, QUAD], F32, name="row_sq", tag="row_sq")
+            junk = work.tile([P, D], BF16, name="junk", tag="junk")
+            nc.scalar.activation(
+                out=junk[:], in_=outs[q][:, a, :], func=FUNC.Square,
+                accum_out=row_sq[q][:, a : a + 1],
+            )
+
+        def st_clamp(q):
+            lo = len(POOL_Z)
+            if lo < QUAD:
+                nc.vector.tensor_scalar(
+                    out=clamped[q][:, lo:QUAD, :], in0=outs[q][:, lo:QUAD, :], scalar1=CLAMP, scalar2=-CLAMP,
+                    op0=ALU.min, op1=ALU.max,
+                )
+
+        def st_guard(q):
+            scaled_sq[q] = small.tile([P, QUAD], F32, name="scaled_sq", tag="scaled_sq")
+            nc.vector.tensor_scalar(
+                out=scaled_sq[q][:], in0=row_sq[q][:], scalar1=EPS * EPS, scalar2=EPS * EPS,
+                op0=ALU.max, op1=ALU.mult,
+            )
+
+        def st_root(q):
+            root[q] = small.tile([P, QUAD], F32, name="root", tag="root")
+            nc.scalar.activation(out=root[q][:], in_=scaled_sq[q][:], func=FUNC.Sqrt)
+
+        def st_recip(q):
+            inv_root[q] = small.tile([P, QUAD], F32, name="inv_root", tag="inv_root")
+            nc.vector.reciprocal(out=inv_root[q][:], in_=root[q][:])
+
+        def st_factor(q):
+            factor[q] = small.tile([P, QUAD], F32, name="factor", tag="factor")
+            nc.vector.tensor_tensor(
+                out=factor[q][:], in0=row_sum[q][:], in1=inv_root[q][:], op=ALU.mult
+            )
+            cs[q] = work.tile([P, QUAD, D], F32, name="cs", tag="cs", bufs=3)
+
+        def st_c(q, a):
+            if a in SCALAR_C and q < LATE:
+                nc.scalar.activation(
+                    out=cs[q][:, a, :], in_=clamped[q][:, a, :], func=FUNC.Copy,
+                    scale=factor[q][:, a : a + 1],
+                )
+            else:
+                nc.vector.tensor_scalar(
+                    out=cs[q][:, a, :], in0=clamped[q][:, a, :], scalar1=factor[q][:, a : a + 1],
+                    scalar2=(-1.0 if a in NEGATED else 1.0), op0=ALU.mult, op1=ALU.mult,
+                )
+            if q == 0 and a == 0:
+                moved = psum.tile([P, D], F32, name="xt", tag="xt", bufs=2)
+                nc.tensor.matmul(
+                    out=moved[:], lhsT=shift[:], rhs=cs[0][:, 0, :], start=True, stop=True
+                )
+                nc.scalar.copy(out=c_next[:], in_=moved[:])
+
+        def st_pairs_on_vector(q):
+            if PE_PAIRS < QUAD:
+                dv[q] = work.tile([P, QUAD - PE_PAIRS, D], F32, name="dv", tag="dv")
+                nc.vector.tensor_tensor(
+                    out=dv[q][:], in0=cs[q][:, PE_PAIRS:QUAD, :], in1=cs[q][:, PE_PAIRS - 1 : QUAD - 1, :],
+                    op=(ALU.add if PE_PAIRS == 3 else ALU.subtract),
+                )
+
+        def st_sum(g, b):
+            cols = slice(b * P, (b + 1) * P)
+            dt = psum.tile([P, QUAD, P], F32, name="dt", tag="dt", bufs=2)
+            first = 1 if g == 0 else 0
+            for s in range(first, QUAD):
+                if s < PE_PAIRS:
+                    before = cs[g - 1][:, QUAD - 1, cols] if s == 0 else cs[g][:, s - 1, cols]
+                    nc.tensor.matmul(
+                        out=dt[:, s, :], lhsT=before, rhs=ident[:],
+                        start=True, stop=False, is_transpose=True,
+                    )
+                    nc.tensor.matmul(
+                        out=dt[:, s, :], lhsT=cs[g][:, s, cols], rhs=ident[:],
+                        start=False, stop=True, is_transpose=True,
+                    )
+                else:
+                    nc.tensor.transpose(
+                        out=dt[:, s, :], in_=dv[g][:, s - PE_PAIRS, cols], identity=ident[:]
+                    )
+            junk = work.tile([P, D], BF16, name="junk", tag="junk")
+            nc.scalar.activation(
+                out=junk[:, first * P : D],
+                in_=dt[:].rearrange("p a r -> p (a r)")[:, first * P : D],
+                func=FUNC.Abs, accum_out=sums[:, b, g : g + 1],
+            )
+
+        def st_last_pair():
+            dt = psum.tile([P, BLOCKS, P], F32, name="dt", tag="dt", bufs=2)
+            for b in range(BLOCKS):
+                cols = slice(b * P, (b + 1) * P)
+                nc.tensor.matmul(
+                    out=dt[:, b, :], lhsT=cs[QUADS - 1][:, QUAD - 1, cols], rhs=ident[:],
+                    start=True, stop=False, is_transpose=True,
+                )
+                nc.tensor.matmul(
+                    out=dt[:, b, :], lhsT=c_next[:, cols], rhs=ident[:],
+                    start=False, stop=True, is_transpose=True,
+                )
+            for b in range(BLOCKS):
+                junk = work.tile([P, D], BF16, name="junk", tag="junk")
+                nc.scalar.activation(
+                    out=junk[:, 0 : P - 1], in_=dt[:, b, 0 : P - 1], func=FUNC.Abs,
+                    accum_out=sums[:, b, QUADS : QUADS + 1],
+                )
+
+        w_grouped = const.tile([P, BLOCKS * D], BF16, name="w_grouped", align_bytes=64)
+        turn_half(w_rows, w_grouped, 0)
+        turn_half(w_rows, w_grouped, 1)
+        w_codes = const.tile([P, D], U32, name="w_codes", align_bytes=64)
+        w_planes = const.tile([P, D], U8, name="w_planes", align_bytes=64)
+        c_next = const.tile([P, D], F32, name="c_next")
+
+        def live(q):
+            return 0 <= q < QUADS
+
+        def st_weights(q):
+            nc.vector.quantize_mx(
+                out=w_codes[:].bitcast(FP8X4), scales=w_planes[:], in_=w_grouped[:]
+            )
+
+        stages = {
+            "widen": st_widen, "turn": st_turn, "quant": st_quantize, "mult": st_multiply, "bias": st_bias,
+            "square": st_square, "clamp": st_clamp, "guard": st_guard, "root": st_root, "recip": st_recip,
+            "factor": st_factor, "c": st_c, "pairs": st_pairs_on_vector, "sum": st_sum,
+        }
+        for i in range(-3, QUADS + 2):
+            for step in ORDER:
+                if step[0] == "wq":
+                    if i == step[1]:
+                        st_weights(0)
+                elif live(i + step[1]):
+                    stages[step[0]](i + step[1], *step[2:])
+        st_last_pair()
+
+        total = const.tile([P, BLOCKS], F32, name="total")
+        nc.vector.tensor_reduce(out=total[:], in_=sums[:], axis=mybir.AxisListType.X, op=ALU.add)
+        spread = psum.tile([P, D], F32, name="mx", tag="mx", bufs=4)
+        for b in range(BLOCKS):
+            nc.tensor.transpose(
+                out=spread[:, b * P : (b + 1) * P],
+                in_=total[:, b : b + 1].to_broadcast([P, P]),
+                identity=ident[:],
+            )
+        result = const.tile([P, D], F32, name="result")
+        nc.vector.tensor_copy(out=result[:, 0 : D // 2], in_=spread[:, 0 : D // 2])
+        nc.scalar.copy(out=result[:, D // 2 : D], in_=spread[:, D // 2 : D])
+        out_view = out.rearrange("(e p) d -> e p d", p=P)
+        for e in range(D // P):
+            if e % 2 == 0:
+                nc.sync.dma_start(out=out_view[e], in_=result[:])
+            else:
+                nc.scalar.dma_start(out=out_view[e], in_=result[:])

@@ -22,7 +22,7 @@ BLOCKS = D // P
 EPS = 1e-8
 CLAMP = EPS / math.sqrt(D)
 
-PE_PAIRS = 3
+PE_PAIRS = 4
 NEGATED = (0, 2)
 SCALAR_C = (1, 3)
 POOL_Z = (0, 1, 2)

@@ -17,17 +17,32 @@ P = 128
 ROWS = 8192
 D = 512
 QUAD = 4
+HALF = 2
 QUADS = ROWS // (P * QUAD)
 BLOCKS = D // P
 EPS = 1e-8
 CLAMP = EPS / math.sqrt(D)
 
-PE_PAIRS = 4
 NEGATED = (0, 2)
-SCALAR_C = (1, 3)
-POOL_Z = (0, 1, 2)
-LATE = 13
-ORDER = (("bias", 0, 0), ("quant", 1), ("turn", 2, 0), ("guard", -1), ("bias", 0, 1), ("sum", -2, 1), ("root", -1), ("bias", 0, 2), ("square", 0, 0), ("recip", -1), ("turn", 2, 1), ("factor", -1), ("bias", 0, 3), ("sum", -2, 0), ("c", -1, 2), ("c", -1, 3), ("widen", 3), ("sum", -2, 2), ("c", -1, 1), ("c", -1, 0), ("square", 0, 1), ("mult", 1), ("square", 0, 2), ("square", 0, 3), ("wq", -3), ("pairs", -1), ("clamp", 0), ("sum", -2, 3))
+SCALAR_C = (3,)
+POOL_Z = (0, 1, 2, 3)
+LATE = 14
+LATE_SQUARES = (3,)
+
+ORDER = (
+    ("bias", 0, 0), ("square", 0, 0), ("sum", -1, 0), ("bias", 0, 1), ("square", 0, 1), ("sum", -1, 1),
+    ("bias", 0, 2), ("square", 0, 2), ("bias", 0, 3), ("square", 0, 3), ("root", 0), ("clamp", 0),
+    ("sum", -1, 2), ("sum", -1, 3),
+    ("widen", 2, 0), ("flip", 2, 0), ("widen", 2, 1), ("flip", 2, 1), ("wq", -2), ("quant", 1), ("mult", 1),
+    ("factor", 0), ("c", 0, 0), ("c", 0, 1), ("c", 0, 2), ("c", 0, 3), ("copy", 2, 0), ("copy", 2, 1), ("next", 0),
+)
+LATE_ORDER = (
+    ("bias", 0, 0), ("square", 0, 0), ("bias", 0, 1), ("square", 0, 1),
+    ("bias", 0, 2), ("square", 0, 2), ("bias", 0, 3), ("square", 0, 3), ("root", 0), ("clamp", 0),
+    ("sum", -1, 0), ("sum", -1, 1), ("quant", 1), ("mult", 1),
+    ("factor", 0), ("c", 0, 0), ("c", 0, 1), ("c", 0, 2), ("c", 0, 3),
+    ("sum", -1, 2), ("sum", -1, 3),
+)
 
 FLOPS = 2 * ROWS * D * D
 
@@ -43,8 +58,8 @@ def tile_dispatcher_pa_kernel(tc, inv_bytes, inv_scale, Wk, bk, out):
         psum = ctx.enter_context(tc.psum_pool(name="psum", bufs=2))
         ctx.enter_context(tc.manual_schedule())
 
-        scale_rep = const.tile([P, QUAD, D], F32, name="scale_rep")
-        nc.sync.dma_start(
+        scale_rep = const.tile([P, HALF, D], F32, name="scale_rep")
+        nc.scalar.dma_start(
             out=scale_rep[:, 0, :],
             in_=inv_scale.rearrange("a b k -> (a b k)").partition_broadcast(P),
         )
@@ -70,7 +85,7 @@ def tile_dispatcher_pa_kernel(tc, inv_bytes, inv_scale, Wk, bk, out):
         one = const.tile([P, 1], F32, name="one")
         nc.vector.memset(one[:], 1.0)
         warm = const.tile([P, 1], F32, name="warm")
-        nc.scalar.activation(out=warm[:], in_=one[:], func=FUNC.Sqrt)
+        nc.scalar.activation(out=warm[:], in_=one[:], func=FUNC.Abs_reciprocal_sqrt)
 
         ident = const.tile([P, P], F32, name="ident")
         make_identity(nc, ident[:])
@@ -78,41 +93,51 @@ def tile_dispatcher_pa_kernel(tc, inv_bytes, inv_scale, Wk, bk, out):
         nc.vector.memset(shift[:], 0.0)
         nc.vector.tensor_copy(out=shift[:, 0 : P - 1], in_=ident[:, 1:P])
         nc.vector.tensor_copy(out=scale_rep[:, 1, :], in_=scale_rep[:, 0, :])
-        nc.vector.tensor_copy(out=scale_rep[:, 2:4, :], in_=scale_rep[:, 0:2, :])
 
         sums = const.tile([P, BLOCKS, QUADS + 1], F32, name="sums")
 
-        wide, grouped, codes, planes = {}, {}, {}, {}
-        banks, outs, clamped, cs, dv = {}, {}, {}, {}, {}
-        row_sum, row_sq, scaled_sq, root, inv_root, factor = {}, {}, {}, {}, {}, {}
+        wide, flipped, grouped, codes, planes = {}, {}, {}, {}, {}
+        banks, outs, clamped, cs = {}, {}, {}, {}
+        row_sum, row_sq, inv_norm, factor = {}, {}, {}, {}
 
-        def turn_half(src, dst, h):
+        def flip_half(src, h):
             sw = src[:].bitcast(F32).rearrange("p (a m u) -> p a m u", a=QUAD, u=2)
-            dw = dst[:].bitcast(F32).rearrange("p (a r u) -> p a r u", a=QUAD, u=2)
             xt = psum.tile([P, 2, 2, P], F32, name="xt", tag="xt", bufs=2)
             for a in range(2):
                 for u in range(2):
                     nc.tensor.transpose(
                         out=xt[:, a, u, :], in_=sw[:, 2 * h + a, :, u], identity=ident[:]
                     )
+            return xt
+
+        def copy_half(xt, dst, h):
+            dw = dst[:].bitcast(F32).rearrange("p (a r u) -> p a r u", a=QUAD, u=2)
             nc.scalar.copy(
                 out=dw[:, 2 * h : 2 * h + 2, :, :],
                 in_=xt[:].rearrange("p a u r -> p a r u"),
             )
 
-        def st_widen(q):
-            wide[q] = work.tile([P, QUAD * D], BF16, name="wide", tag="wide", align_bytes=64)
+        def turn_half(src, dst, h):
+            copy_half(flip_half(src, h), dst, h)
+
+        def st_widen(q, h):
+            if h == 0:
+                wide[q] = work.tile([P, QUAD * D], BF16, name="wide", tag="wide", align_bytes=64)
+            cols = slice(h * HALF * D, (h + 1) * HALF * D)
             nc.vector.tensor_tensor(
-                out=wide[q][:],
-                in0=byte_tiles[q][:].bitcast(FP8),
+                out=wide[q][:, cols],
+                in0=byte_tiles[q][:, cols].bitcast(FP8),
                 in1=scale_rep[:].rearrange("p a k -> p (a k)"),
                 op=ALU.mult,
             )
 
-        def st_turn(q, h):
+        def st_flip(q, h):
+            flipped[(q, h)] = flip_half(wide[q], h)
+
+        def st_copy(q, h):
             if h == 0:
                 grouped[q] = work.tile([P, QUAD * D], BF16, name="grouped", tag="grouped", align_bytes=64)
-            turn_half(wide[q], grouped[q], h)
+            copy_half(flipped[(q, h)], grouped[q], h)
 
         def st_quantize(q):
             codes[q] = work.tile([P, QUAD * P], U32, name="x_codes", tag="x_codes", align_bytes=64)
@@ -152,6 +177,13 @@ def tile_dispatcher_pa_kernel(tc, inv_bytes, inv_scale, Wk, bk, out):
         def st_square(q, a):
             if a == 0:
                 row_sq[q] = small.tile([P, QUAD], F32, name="row_sq", tag="row_sq")
+            if q >= LATE and a in LATE_SQUARES:
+                junk_v = work.tile([P, D], BF16, name="junk_v", tag="junk_v")
+                nc.vector.scalar_tensor_tensor(
+                    out=junk_v[:], in0=outs[q][:, a, :], scalar=1.0, in1=outs[q][:, a, :],
+                    op0=ALU.mult, op1=ALU.mult, accum_out=row_sq[q][:, a : a + 1],
+                )
+                return
             junk = work.tile([P, D], BF16, name="junk", tag="junk")
             nc.scalar.activation(
                 out=junk[:], in_=outs[q][:, a, :], func=FUNC.Square,
@@ -166,25 +198,17 @@ def tile_dispatcher_pa_kernel(tc, inv_bytes, inv_scale, Wk, bk, out):
                     op0=ALU.min, op1=ALU.max,
                 )
 
-        def st_guard(q):
-            scaled_sq[q] = small.tile([P, QUAD], F32, name="scaled_sq", tag="scaled_sq")
-            nc.vector.tensor_scalar(
-                out=scaled_sq[q][:], in0=row_sq[q][:], scalar1=EPS * EPS, scalar2=EPS * EPS,
-                op0=ALU.max, op1=ALU.mult,
-            )
-
         def st_root(q):
-            root[q] = small.tile([P, QUAD], F32, name="root", tag="root")
-            nc.scalar.activation(out=root[q][:], in_=scaled_sq[q][:], func=FUNC.Sqrt)
-
-        def st_recip(q):
-            inv_root[q] = small.tile([P, QUAD], F32, name="inv_root", tag="inv_root")
-            nc.vector.reciprocal(out=inv_root[q][:], in_=root[q][:])
+            inv_norm[q] = small.tile([P, QUAD], F32, name="inv_norm", tag="inv_norm")
+            nc.scalar.activation(
+                out=inv_norm[q][:], in_=row_sq[q][:], func=FUNC.Abs_reciprocal_sqrt, scale=EPS * EPS
+            )
 
         def st_factor(q):
             factor[q] = small.tile([P, QUAD], F32, name="factor", tag="factor")
-            nc.vector.tensor_tensor(
-                out=factor[q][:], in0=row_sum[q][:], in1=inv_root[q][:], op=ALU.mult
+            nc.vector.scalar_tensor_tensor(
+                out=factor[q][:], in0=inv_norm[q][:], scalar=1.0 / (EPS * EPS), in1=row_sum[q][:],
+                op0=ALU.min, op1=ALU.mult,
             )
             cs[q] = work.tile([P, QUAD, D], F32, name="cs", tag="cs", bufs=3)
 
@@ -199,40 +223,32 @@ def tile_dispatcher_pa_kernel(tc, inv_bytes, inv_scale, Wk, bk, out):
                     out=cs[q][:, a, :], in0=clamped[q][:, a, :], scalar1=factor[q][:, a : a + 1],
                     scalar2=(-1.0 if a in NEGATED else 1.0), op0=ALU.mult, op1=ALU.mult,
                 )
-            if q == 0 and a == 0:
-                moved = psum.tile([P, D], F32, name="xt", tag="xt", bufs=2)
+
+        def st_next(q):
+            if q == 0:
+                moved = psum.tile([P, D], F32, name="dt", tag="dt", bufs=2)
                 nc.tensor.matmul(
                     out=moved[:], lhsT=shift[:], rhs=cs[0][:, 0, :], start=True, stop=True
                 )
                 nc.scalar.copy(out=c_next[:], in_=moved[:])
 
-        def st_pairs_on_vector(q):
-            if PE_PAIRS < QUAD:
-                dv[q] = work.tile([P, QUAD - PE_PAIRS, D], F32, name="dv", tag="dv")
-                nc.vector.tensor_tensor(
-                    out=dv[q][:], in0=cs[q][:, PE_PAIRS:QUAD, :], in1=cs[q][:, PE_PAIRS - 1 : QUAD - 1, :],
-                    op=(ALU.add if PE_PAIRS == 3 else ALU.subtract),
-                )
-
         def st_sum(g, b):
             cols = slice(b * P, (b + 1) * P)
-            dt = psum.tile([P, QUAD, P], F32, name="dt", tag="dt", bufs=2)
+            if g == QUADS - 1:
+                dt = psum.tile([P, QUAD, P], F32, name="mx", tag="mx", bufs=4)
+            else:
+                dt = psum.tile([P, QUAD, P], F32, name="dt", tag="dt", bufs=2)
             first = 1 if g == 0 else 0
             for s in range(first, QUAD):
-                if s < PE_PAIRS:
-                    before = cs[g - 1][:, QUAD - 1, cols] if s == 0 else cs[g][:, s - 1, cols]
-                    nc.tensor.matmul(
-                        out=dt[:, s, :], lhsT=before, rhs=ident[:],
-                        start=True, stop=False, is_transpose=True,
-                    )
-                    nc.tensor.matmul(
-                        out=dt[:, s, :], lhsT=cs[g][:, s, cols], rhs=ident[:],
-                        start=False, stop=True, is_transpose=True,
-                    )
-                else:
-                    nc.tensor.transpose(
-                        out=dt[:, s, :], in_=dv[g][:, s - PE_PAIRS, cols], identity=ident[:]
-                    )
+                before = cs[g - 1][:, QUAD - 1, cols] if s == 0 else cs[g][:, s - 1, cols]
+                nc.tensor.matmul(
+                    out=dt[:, s, :], lhsT=before, rhs=ident[:],
+                    start=True, stop=False, is_transpose=True,
+                )
+                nc.tensor.matmul(
+                    out=dt[:, s, :], lhsT=cs[g][:, s, cols], rhs=ident[:],
+                    start=False, stop=True, is_transpose=True,
+                )
             junk = work.tile([P, D], BF16, name="junk", tag="junk")
             nc.scalar.activation(
                 out=junk[:, first * P : D],
@@ -275,12 +291,12 @@ def tile_dispatcher_pa_kernel(tc, inv_bytes, inv_scale, Wk, bk, out):
             )
 
         stages = {
-            "widen": st_widen, "turn": st_turn, "quant": st_quantize, "mult": st_multiply, "bias": st_bias,
-            "square": st_square, "clamp": st_clamp, "guard": st_guard, "root": st_root, "recip": st_recip,
-            "factor": st_factor, "c": st_c, "pairs": st_pairs_on_vector, "sum": st_sum,
+            "widen": st_widen, "flip": st_flip, "copy": st_copy, "quant": st_quantize, "mult": st_multiply, "bias": st_bias,
+            "square": st_square, "clamp": st_clamp, "root": st_root,
+            "factor": st_factor, "c": st_c, "sum": st_sum, "next": st_next,
         }
-        for i in range(-3, QUADS + 2):
-            for step in ORDER:
+        for i in range(-2, QUADS + 1):
+            for step in (ORDER if i < LATE else LATE_ORDER):
                 if step[0] == "wq":
                     if i == step[1]:
                         st_weights(0)

@@ -24,24 +24,33 @@ EPS = 1e-8
 CLAMP = EPS / math.sqrt(D)
 
 NEGATED = (0, 2)
-SCALAR_C = (3,)
-POOL_Z = (0, 1, 2, 3)
+SCALAR_C = (1,)
 LATE = 14
 LATE_SQUARES = (3,)
 
 ORDER = (
-    ("bias", 0, 0), ("square", 0, 0), ("sum", -1, 0), ("bias", 0, 1), ("square", 0, 1), ("sum", -1, 1),
-    ("bias", 0, 2), ("square", 0, 2), ("bias", 0, 3), ("square", 0, 3), ("root", 0), ("clamp", 0),
-    ("sum", -1, 2), ("sum", -1, 3),
-    ("widen", 2, 0), ("flip", 2, 0), ("widen", 2, 1), ("flip", 2, 1), ("wq", -2), ("quant", 1), ("mult", 1),
-    ("factor", 0), ("c", 0, 0), ("c", 0, 1), ("c", 0, 2), ("c", 0, 3), ("copy", 2, 0), ("copy", 2, 1), ("next", 0),
+    ("bias", 0, 0), ("square", 0, 0), ("copy", 1, 0), ("copy", 1, 1), ("bias", 0, 1), ("square", 0, 1), ("sum", -2, 0),
+    ("bias", 0, 2), ("square", 0, 2), ("sum", -2, 1), ("bias", 0, 3), ("square", 0, 3), ("root", 0),
+    ("factor", -1), ("c", -1, 1), ("quant", 1), ("mult", 1), ("sum", -2, 2), ("sum", -2, 3),
+    ("widen", 2, 0), ("flip", 2, 0), ("widen", 2, 1), ("flip", 2, 1),
+    ("c", -1, 0), ("c", -1, 2), ("c", -1, 3), ("clamp", 0),
+)
+FILL_ORDER = (
+    ("copy", 1, 0), ("copy", 1, 1), ("widen", 2, 0), ("flip", 2, 0), ("quant", 1), ("mult", 1), ("widen", 2, 1), ("flip", 2, 1), ("wq", -2),
+)
+TURN_ORDER = (
+    ("bias", 0, 0), ("square", 0, 0), ("copy", 1, 0), ("copy", 1, 1), ("bias", 0, 1), ("square", 0, 1), ("sum", -2, 0),
+    ("bias", 0, 2), ("square", 0, 2), ("sum", -2, 1), ("bias", 0, 3), ("square", 0, 3), ("root", 0),
+    ("factor", -1), ("c", -1, 1), ("quant", 1), ("mult", 1), ("sum", -2, 2), ("sum", -2, 3),
+    ("c", -1, 0), ("c", -1, 2), ("c", -1, 3), ("clamp", 0),
+    ("factor", 0), ("c", 0, 0), ("c", 0, 1), ("c", 0, 2), ("c", 0, 3),
+    ("sum", -1, 0), ("sum", -1, 1), ("sum", -1, 2), ("sum", -1, 3),
 )
 LATE_ORDER = (
     ("bias", 0, 0), ("square", 0, 0), ("bias", 0, 1), ("square", 0, 1),
     ("bias", 0, 2), ("square", 0, 2), ("bias", 0, 3), ("square", 0, 3), ("root", 0), ("clamp", 0),
-    ("sum", -1, 0), ("sum", -1, 1), ("quant", 1), ("mult", 1),
+    ("sum", -1, 0), ("sum", -1, 1), ("sum", -1, 2), ("sum", -1, 3),
     ("factor", 0), ("c", 0, 0), ("c", 0, 1), ("c", 0, 2), ("c", 0, 3),
-    ("sum", -1, 2), ("sum", -1, 3),
 )
 
 FLOPS = 2 * ROWS * D * D
@@ -89,9 +98,9 @@ def tile_dispatcher_pa_kernel(tc, inv_bytes, inv_scale, Wk, bk, out):
 
         ident = const.tile([P, P], F32, name="ident")
         make_identity(nc, ident[:])
-        shift = const.tile([P, P], F32, name="shift")
-        nc.vector.memset(shift[:], 0.0)
-        nc.vector.tensor_copy(out=shift[:, 0 : P - 1], in_=ident[:, 1:P])
+        rotate = const.tile([P, P], F32, name="rotate")
+        nc.vector.tensor_copy(out=rotate[:, 0 : P - 1], in_=ident[:, 1:P])
+        nc.vector.tensor_copy(out=rotate[:, P - 1 : P], in_=ident[:, 0:1])
         nc.vector.tensor_copy(out=scale_rep[:, 1, :], in_=scale_rep[:, 0, :])
 
         sums = const.tile([P, BLOCKS, QUADS + 1], F32, name="sums")
@@ -163,16 +172,10 @@ def tile_dispatcher_pa_kernel(tc, inv_bytes, inv_scale, Wk, bk, out):
             if a == 0:
                 outs[q] = work.tile([P, QUAD, D], F32, name="outs", tag="outs")
                 row_sum[q] = small.tile([P, QUAD], F32, name="row_sum", tag="row_sum")
-                clamped[q] = work.tile([P, QUAD, D], F32, name="clamped", tag="clamped")
             nc.vector.scalar_tensor_tensor(
                 out=outs[q][:, a, :], in0=banks[(q, a)][:], scalar=1.0, in1=bias_rep[:],
                 op0=ALU.mult, op1=ALU.add, accum_out=row_sum[q][:, a : a + 1],
             )
-            if a in POOL_Z:
-                nc.gpsimd.tensor_scalar(
-                    out=clamped[q][:, a, :], in0=outs[q][:, a, :], scalar1=CLAMP, scalar2=-CLAMP,
-                    op0=ALU.min, op1=ALU.max,
-                )
 
         def st_square(q, a):
             if a == 0:
@@ -191,12 +194,12 @@ def tile_dispatcher_pa_kernel(tc, inv_bytes, inv_scale, Wk, bk, out):
             )
 
         def st_clamp(q):
-            lo = len(POOL_Z)
-            if lo < QUAD:
-                nc.vector.tensor_scalar(
-                    out=clamped[q][:, lo:QUAD, :], in0=outs[q][:, lo:QUAD, :], scalar1=CLAMP, scalar2=-CLAMP,
-                    op0=ALU.min, op1=ALU.max,
-                )
+            clamped[q] = work.tile([P, QUAD, D], F32, name="clamped", tag="clamped", bufs=1)
+            engine = nc.gpsimd if q < LATE else nc.vector
+            engine.tensor_scalar(
+                out=clamped[q][:], in0=outs[q][:], scalar1=CLAMP, scalar2=-CLAMP,
+                op0=ALU.min, op1=ALU.max,
+            )
 
         def st_root(q):
             inv_norm[q] = small.tile([P, QUAD], F32, name="inv_norm", tag="inv_norm")
@@ -212,41 +215,38 @@ def tile_dispatcher_pa_kernel(tc, inv_bytes, inv_scale, Wk, bk, out):
             )
             cs[q] = work.tile([P, QUAD, D], F32, name="cs", tag="cs", bufs=3)
 
+        def c_of(q, a):
+            return c_first[:] if (q == 0 and a == 0) else cs[q][:, a, :]
+
         def st_c(q, a):
             if a in SCALAR_C and q < LATE:
                 nc.scalar.activation(
-                    out=cs[q][:, a, :], in_=clamped[q][:, a, :], func=FUNC.Copy,
+                    out=c_of(q, a), in_=clamped[q][:, a, :], func=FUNC.Copy,
                     scale=factor[q][:, a : a + 1],
                 )
             else:
                 nc.vector.tensor_scalar(
-                    out=cs[q][:, a, :], in0=clamped[q][:, a, :], scalar1=factor[q][:, a : a + 1],
+                    out=c_of(q, a), in0=clamped[q][:, a, :], scalar1=factor[q][:, a : a + 1],
                     scalar2=(-1.0 if a in NEGATED else 1.0), op0=ALU.mult, op1=ALU.mult,
                 )
-
-        def st_next(q):
-            if q == 0:
-                moved = psum.tile([P, D], F32, name="dt", tag="dt", bufs=2)
-                nc.tensor.matmul(
-                    out=moved[:], lhsT=shift[:], rhs=cs[0][:, 0, :], start=True, stop=True
-                )
-                nc.scalar.copy(out=c_next[:], in_=moved[:])
 
         def st_sum(g, b):
             cols = slice(b * P, (b + 1) * P)
             if g == QUADS - 1:
                 dt = psum.tile([P, QUAD, P], F32, name="mx", tag="mx", bufs=4)
+            elif g >= LATE - 1 and b >= 2:
+                dt = psum.tile([P, QUAD, P], F32, name="xt", tag="xt", bufs=2)
             else:
                 dt = psum.tile([P, QUAD, P], F32, name="dt", tag="dt", bufs=2)
             first = 1 if g == 0 else 0
             for s in range(first, QUAD):
-                before = cs[g - 1][:, QUAD - 1, cols] if s == 0 else cs[g][:, s - 1, cols]
+                before = c_of(g - 1, QUAD - 1) if s == 0 else c_of(g, s - 1)
                 nc.tensor.matmul(
-                    out=dt[:, s, :], lhsT=before, rhs=ident[:],
+                    out=dt[:, s, :], lhsT=before[:, cols], rhs=ident[:],
                     start=True, stop=False, is_transpose=True,
                 )
                 nc.tensor.matmul(
-                    out=dt[:, s, :], lhsT=cs[g][:, s, cols], rhs=ident[:],
+                    out=dt[:, s, :], lhsT=c_of(g, s)[:, cols], rhs=ident[:],
                     start=False, stop=True, is_transpose=True,
                 )
             junk = work.tile([P, D], BF16, name="junk", tag="junk")
@@ -261,11 +261,11 @@ def tile_dispatcher_pa_kernel(tc, inv_bytes, inv_scale, Wk, bk, out):
             for b in range(BLOCKS):
                 cols = slice(b * P, (b + 1) * P)
                 nc.tensor.matmul(
-                    out=dt[:, b, :], lhsT=cs[QUADS - 1][:, QUAD - 1, cols], rhs=ident[:],
+                    out=dt[:, b, :], lhsT=c_first[:, cols], rhs=rotate[:],
                     start=True, stop=False, is_transpose=True,
                 )
                 nc.tensor.matmul(
-                    out=dt[:, b, :], lhsT=c_next[:, cols], rhs=ident[:],
+                    out=dt[:, b, :], lhsT=cs[QUADS - 1][:, QUAD - 1, cols], rhs=ident[:],
                     start=False, stop=True, is_transpose=True,
                 )
             for b in range(BLOCKS):
@@ -280,7 +280,7 @@ def tile_dispatcher_pa_kernel(tc, inv_bytes, inv_scale, Wk, bk, out):
         turn_half(w_rows, w_grouped, 1)
         w_codes = const.tile([P, D], U32, name="w_codes", align_bytes=64)
         w_planes = const.tile([P, D], U8, name="w_planes", align_bytes=64)
-        c_next = const.tile([P, D], F32, name="c_next")
+        c_first = const.tile([P, D], F32, name="c_first")
 
         def live(q):
             return 0 <= q < QUADS
@@ -293,10 +293,10 @@ def tile_dispatcher_pa_kernel(tc, inv_bytes, inv_scale, Wk, bk, out):
         stages = {
             "widen": st_widen, "flip": st_flip, "copy": st_copy, "quant": st_quantize, "mult": st_multiply, "bias": st_bias,
             "square": st_square, "clamp": st_clamp, "root": st_root,
-            "factor": st_factor, "c": st_c, "sum": st_sum, "next": st_next,
+            "factor": st_factor, "c": st_c, "sum": st_sum,
         }
         for i in range(-2, QUADS + 1):
-            for step in (ORDER if i < LATE else LATE_ORDER):
+            for step in (FILL_ORDER if i < 0 else ORDER if i < LATE else TURN_ORDER if i == LATE else LATE_ORDER):
                 if step[0] == "wq":
                     if i == step[1]:
                         st_weights(0)

@@ -29,19 +29,18 @@ LATE = 14
 LATE_SQUARES = (3,)
 
 ORDER = (
-    ("bias", 0, 0), ("square", 0, 0), ("copy", 1, 0), ("copy", 1, 1), ("bias", 0, 1), ("square", 0, 1), ("sum", -2, 0),
-    ("bias", 0, 2), ("square", 0, 2), ("sum", -2, 1), ("bias", 0, 3), ("square", 0, 3), ("root", 0),
-    ("factor", -1), ("c", -1, 1), ("quant", 1), ("mult", 1), ("sum", -2, 2), ("sum", -2, 3),
-    ("widen", 2, 0), ("flip", 2, 0), ("widen", 2, 1), ("flip", 2, 1),
-    ("c", -1, 0), ("c", -1, 2), ("c", -1, 3), ("clamp", 0),
+    ("bias", 0, 0), ("square", 0, 0), ("sum", -2, 0), ("bias", 0, 1), ("square", 0, 1), ("sum", -2, 1),
+    ("bias", 0, 2), ("square", 0, 2), ("sum", -2, 2), ("bias", 0, 3), ("square", 0, 3), ("root", 0),
+    ("widen", 2, 0), ("widen", 2, 1), ("factor", -1), ("c", -1, 1), ("sum", -2, 3), ("flip", 2, 0), ("flip", 2, 1),
+    ("quant", 1), ("mult", 1), ("c", -1, 0), ("c", -1, 2), ("c", -1, 3), ("clamp", 0), ("copy", 2, 0), ("copy", 2, 1),
 )
 FILL_ORDER = (
-    ("copy", 1, 0), ("copy", 1, 1), ("widen", 2, 0), ("flip", 2, 0), ("quant", 1), ("mult", 1), ("widen", 2, 1), ("flip", 2, 1), ("wq", -2),
+    ("widen", 2, 0), ("flip", 2, 0), ("copy", 2, 0), ("quant", 1), ("mult", 1), ("widen", 2, 1), ("flip", 2, 1), ("copy", 2, 1), ("wq", -2),
 )
 TURN_ORDER = (
-    ("bias", 0, 0), ("square", 0, 0), ("copy", 1, 0), ("copy", 1, 1), ("bias", 0, 1), ("square", 0, 1), ("sum", -2, 0),
-    ("bias", 0, 2), ("square", 0, 2), ("sum", -2, 1), ("bias", 0, 3), ("square", 0, 3), ("root", 0),
-    ("factor", -1), ("c", -1, 1), ("quant", 1), ("mult", 1), ("sum", -2, 2), ("sum", -2, 3),
+    ("bias", 0, 0), ("square", 0, 0), ("sum", -2, 0), ("bias", 0, 1), ("square", 0, 1), ("sum", -2, 1),
+    ("bias", 0, 2), ("square", 0, 2), ("sum", -2, 2), ("bias", 0, 3), ("square", 0, 3), ("root", 0),
+    ("factor", -1), ("c", -1, 1), ("sum", -2, 3), ("quant", 1), ("mult", 1),
     ("c", -1, 0), ("c", -1, 2), ("c", -1, 3), ("clamp", 0),
     ("factor", 0), ("c", 0, 0), ("c", 0, 1), ("c", 0, 2), ("c", 0, 3),
     ("sum", -1, 0), ("sum", -1, 1), ("sum", -1, 2), ("sum", -1, 3),
@@ -111,7 +110,7 @@ def tile_dispatcher_pa_kernel(tc, inv_bytes, inv_scale, Wk, bk, out):
 
         def flip_half(src, h):
             sw = src[:].bitcast(F32).rearrange("p (a m u) -> p a m u", a=QUAD, u=2)
-            xt = psum.tile([P, 2, 2, P], F32, name="xt", tag="xt", bufs=2)
+            xt = psum.tile([P, 2, 2, P], F32, name="tp", tag="tp", bufs=4)
             for a in range(2):
                 for u in range(2):
                     nc.tensor.transpose(
@@ -234,10 +233,8 @@ def tile_dispatcher_pa_kernel(tc, inv_bytes, inv_scale, Wk, bk, out):
             cols = slice(b * P, (b + 1) * P)
             if g == QUADS - 1:
                 dt = psum.tile([P, QUAD, P], F32, name="mx", tag="mx", bufs=4)
-            elif g >= LATE - 1 and b >= 2:
-                dt = psum.tile([P, QUAD, P], F32, name="xt", tag="xt", bufs=2)
             else:
-                dt = psum.tile([P, QUAD, P], F32, name="dt", tag="dt", bufs=2)
+                dt = psum.tile([P, QUAD, P], F32, name="tp", tag="tp", bufs=4)
             first = 1 if g == 0 else 0
             for s in range(first, QUAD):
                 before = c_of(g - 1, QUAD - 1) if s == 0 else c_of(g, s - 1)
@@ -257,7 +254,7 @@ def tile_dispatcher_pa_kernel(tc, inv_bytes, inv_scale, Wk, bk, out):
             )
 
         def st_last_pair():
-            dt = psum.tile([P, BLOCKS, P], F32, name="dt", tag="dt", bufs=2)
+            dt = psum.tile([P, BLOCKS, P], F32, name="tp", tag="tp", bufs=4)
             for b in range(BLOCKS):
                 cols = slice(b * P, (b + 1) * P)
                 nc.tensor.matmul(

@@ -30,17 +30,18 @@ LATE_SQUARES = (3,)
 
 ORDER = (
     ("bias", 0, 0), ("square", 0, 0), ("sum", -2, 0), ("bias", 0, 1), ("square", 0, 1), ("sum", -2, 1),
-    ("bias", 0, 2), ("square", 0, 2), ("sum", -2, 2), ("bias", 0, 3), ("square", 0, 3), ("root", 0),
-    ("widen", 2, 0), ("widen", 2, 1), ("factor", -1), ("c", -1, 1), ("sum", -2, 3), ("flip", 2, 0), ("flip", 2, 1),
-    ("quant", 1), ("mult", 1), ("c", -1, 0), ("c", -1, 2), ("c", -1, 3), ("clamp", 0), ("copy", 2, 0), ("copy", 2, 1),
+    ("bias", 0, 2), ("square", 0, 2), ("bias", 0, 3), ("factor", -1), ("c", -1, 1), ("sum", -2, 2), ("square", 0, 3), ("root", 0),
+    ("quant", 1), ("mult", 1), ("sum", -2, 3),
+    ("widen", 3, 0), ("widen", 3, 1), ("flip", 3, 0), ("flip", 3, 1),
+    ("c", -1, 0), ("c", -1, 2), ("c", -1, 3), ("clamp", 0), ("copy", 3, 0), ("copy", 3, 1),
 )
 FILL_ORDER = (
-    ("widen", 2, 0), ("flip", 2, 0), ("copy", 2, 0), ("quant", 1), ("mult", 1), ("widen", 2, 1), ("flip", 2, 1), ("copy", 2, 1), ("wq", -2),
+    ("quant", 1), ("mult", 1), ("widen", 3, 0), ("flip", 3, 0), ("copy", 3, 0), ("widen", 3, 1), ("flip", 3, 1), ("copy", 3, 1), ("wq", -3),
 )
 TURN_ORDER = (
-    ("bias", 0, 0), ("square", 0, 0), ("sum", -2, 0), ("bias", 0, 1), ("square", 0, 1), ("sum", -2, 1),
+    ("bias", 0, 0), ("square", 0, 0),  ("sum", -2, 0), ("bias", 0, 1), ("square", 0, 1), ("sum", -2, 1),
     ("bias", 0, 2), ("square", 0, 2), ("sum", -2, 2), ("bias", 0, 3), ("square", 0, 3), ("root", 0),
-    ("factor", -1), ("c", -1, 1), ("sum", -2, 3), ("quant", 1), ("mult", 1),
+    ("factor", -1), ("quant", 1), ("mult", 1), ("c", -1, 1), ("sum", -2, 3),
     ("c", -1, 0), ("c", -1, 2), ("c", -1, 3), ("clamp", 0),
     ("factor", 0), ("c", 0, 0), ("c", 0, 1), ("c", 0, 2), ("c", 0, 3),
     ("sum", -1, 0), ("sum", -1, 1), ("sum", -1, 2), ("sum", -1, 3),
@@ -144,7 +145,7 @@ def tile_dispatcher_pa_kernel(tc, inv_bytes, inv_scale, Wk, bk, out):
 
         def st_copy(q, h):
             if h == 0:
-                grouped[q] = work.tile([P, QUAD * D], BF16, name="grouped", tag="grouped", align_bytes=64)
+                grouped[q] = work.tile([P, QUAD * D], BF16, name="grouped", tag="grouped", bufs=3, align_bytes=64)
             copy_half(flipped[(q, h)], grouped[q], h)
 
         def st_quantize(q):
@@ -292,7 +293,7 @@ def tile_dispatcher_pa_kernel(tc, inv_bytes, inv_scale, Wk, bk, out):
             "square": st_square, "clamp": st_clamp, "root": st_root,
             "factor": st_factor, "c": st_c, "sum": st_sum,
         }
-        for i in range(-2, QUADS + 1):
+        for i in range(-3, QUADS + 1):
             for step in (FILL_ORDER if i < 0 else ORDER if i < LATE else TURN_ORDER if i == LATE else LATE_ORDER):
                 if step[0] == "wq":
                     if i == step[1]:

@@ -23,6 +23,7 @@ BLOCKS = D // P
 EPS = 1e-8
 CLAMP = EPS / math.sqrt(D)
 
+PE_PAIRS = (4, 4, 4, 4, 4, 4, 4, 4, 4, 4, 4, 3, 3, 3, 4, 4)
 NEGATED = (0, 2)
 SCALAR_C = (1,)
 LATE = 14
@@ -33,7 +34,7 @@ ORDER = (
     ("bias", 0, 2), ("square", 0, 2), ("bias", 0, 3), ("factor", -1), ("c", -1, 1), ("sum", -2, 2), ("square", 0, 3), ("root", 0),
     ("quant", 1), ("mult", 1), ("sum", -2, 3),
     ("widen", 3, 0), ("widen", 3, 1), ("flip", 3, 0), ("flip", 3, 1),
-    ("c", -1, 0), ("c", -1, 2), ("c", -1, 3), ("clamp", 0), ("copy", 3, 0), ("copy", 3, 1),
+    ("c", -1, 2), ("c", -1, 3), ("c", -1, 0), ("clamp", 0), ("pairs", -1), ("copy", 3, 0), ("copy", 3, 1),
 )
 FILL_ORDER = (
     ("quant", 1), ("mult", 1), ("widen", 3, 0), ("flip", 3, 0), ("copy", 3, 0), ("widen", 3, 1), ("flip", 3, 1), ("copy", 3, 1), ("wq", -3),
@@ -42,15 +43,15 @@ TURN_ORDER = (
     ("bias", 0, 0), ("square", 0, 0),  ("sum", -2, 0), ("bias", 0, 1), ("square", 0, 1), ("sum", -2, 1),
     ("bias", 0, 2), ("square", 0, 2), ("sum", -2, 2), ("bias", 0, 3), ("square", 0, 3), ("root", 0),
     ("factor", -1), ("quant", 1), ("mult", 1), ("c", -1, 1), ("sum", -2, 3),
-    ("c", -1, 0), ("c", -1, 2), ("c", -1, 3), ("clamp", 0),
-    ("factor", 0), ("c", 0, 0), ("c", 0, 1), ("c", 0, 2), ("c", 0, 3),
+    ("c", -1, 2), ("c", -1, 3), ("c", -1, 0), ("pairs", -1), ("clamp", 0),
+    ("factor", 0), ("c", 0, 1), ("c", 0, 2), ("c", 0, 3), ("c", 0, 0), ("pairs", 0),
     ("sum", -1, 0), ("sum", -1, 1), ("sum", -1, 2), ("sum", -1, 3),
 )
 LATE_ORDER = (
     ("bias", 0, 0), ("square", 0, 0), ("bias", 0, 1), ("square", 0, 1),
     ("bias", 0, 2), ("square", 0, 2), ("bias", 0, 3), ("square", 0, 3), ("root", 0), ("clamp", 0),
     ("sum", -1, 0), ("sum", -1, 1), ("sum", -1, 2), ("sum", -1, 3),
-    ("factor", 0), ("c", 0, 0), ("c", 0, 1), ("c", 0, 2), ("c", 0, 3),
+    ("factor", 0), ("c", 0, 3), ("last", 0), ("c", 0, 2), ("c", 0, 1), ("c", 0, 0), ("half", 0),
 )
 
 FLOPS = 2 * ROWS * D * D
@@ -73,12 +74,7 @@ def tile_dispatcher_pa_kernel(tc, inv_bytes, inv_scale, Wk, bk, out):
             in_=inv_scale.rearrange("a b k -> (a b k)").partition_broadcast(P),
         )
         w_rows = const.tile([P, BLOCKS * D], BF16, name="w_rows")
-        nc.scalar.dma_start(
-            out=w_rows[:].rearrange("n (a k) -> n a k", a=BLOCKS),
-            in_=Wk.rearrange("(a n) k -> n a k", n=P),
-        )
         bias_rep = const.tile([P, D], BF16, name="bias_rep")
-        nc.scalar.dma_start(out=bias_rep[:], in_=bk.partition_broadcast(P))
 
         bytes_view = inv_bytes.rearrange("b t k -> (b t) k").rearrange(
             "(p j) k -> p (j k)", p=P
@@ -90,6 +86,13 @@ def tile_dispatcher_pa_kernel(tc, inv_bytes, inv_scale, Wk, bk, out):
                 out=byte_tiles[q][:],
                 in_=bytes_view[:, q * QUAD * D : (q + 1) * QUAD * D],
             )
+            if q == 0:
+                nc.sync.dma_start(
+                    out=w_rows[:].rearrange("n (a k) -> n a k", a=BLOCKS),
+                    in_=Wk.rearrange("(a n) k -> n a k", n=P),
+                )
+            if q == 2:
+                nc.sync.dma_start(out=bias_rep[:], in_=bk.partition_broadcast(P))
 
         one = const.tile([P, 1], F32, name="one")
         nc.vector.memset(one[:], 1.0)
@@ -106,7 +109,7 @@ def tile_dispatcher_pa_kernel(tc, inv_bytes, inv_scale, Wk, bk, out):
         sums = const.tile([P, BLOCKS, QUADS + 1], F32, name="sums")
 
         wide, flipped, grouped, codes, planes = {}, {}, {}, {}, {}
-        banks, outs, clamped, cs = {}, {}, {}, {}
+        banks, outs, clamped, cs, dv, dv_last = {}, {}, {}, {}, {}, {}
         row_sum, row_sq, inv_norm, factor = {}, {}, {}, {}
 
         def flip_half(src, h):
@@ -219,7 +222,7 @@ def tile_dispatcher_pa_kernel(tc, inv_bytes, inv_scale, Wk, bk, out):
             return c_first[:] if (q == 0 and a == 0) else cs[q][:, a, :]
 
         def st_c(q, a):
-            if a in SCALAR_C and q < LATE:
+            if a in SCALAR_C and q < LATE - 1:
                 nc.scalar.activation(
                     out=c_of(q, a), in_=clamped[q][:, a, :], func=FUNC.Copy,
                     scale=factor[q][:, a : a + 1],
@@ -230,6 +233,24 @@ def tile_dispatcher_pa_kernel(tc, inv_bytes, inv_scale, Wk, bk, out):
                     scalar2=(-1.0 if a in NEGATED else 1.0), op0=ALU.mult, op1=ALU.mult,
                 )
 
+        def st_pairs(q):
+            lo = PE_PAIRS[q]
+            if lo < QUAD:
+                dv[q] = work.tile([P, QUAD - 1, D], F32, name="dv", tag="dv")
+                nc.vector.tensor_tensor(
+                    out=dv[q][:, lo - 1 : QUAD - 1, :], in0=cs[q][:, lo:QUAD, :], in1=cs[q][:, lo - 1 : QUAD - 1, :], op=ALU.add,
+                )
+
+        def st_half_pairs(q):
+            half = slice(D // 2, D)
+            dv_last[0] = work.tile([P, QUAD, D // 2], F32, name="dv_last", tag="dv_last", bufs=1)
+            nc.vector.tensor_tensor(
+                out=dv_last[0][:, 1:QUAD, :], in0=cs[q][:, 1:QUAD, half], in1=cs[q][:, 0 : QUAD - 1, half], op=ALU.add,
+            )
+            nc.vector.tensor_tensor(
+                out=dv_last[0][:, 0, :], in0=cs[q][:, 0, half], in1=cs[q - 1][:, QUAD - 1, half], op=ALU.add,
+            )
+
         def st_sum(g, b):
             cols = slice(b * P, (b + 1) * P)
             if g == QUADS - 1:
@@ -237,7 +258,15 @@ def tile_dispatcher_pa_kernel(tc, inv_bytes, inv_scale, Wk, bk, out):
             else:
                 dt = psum.tile([P, QUAD, P], F32, name="tp", tag="tp", bufs=4)
             first = 1 if g == 0 else 0
-            for s in range(first, QUAD):
+            by_vector = g == QUADS - 1 and b >= BLOCKS // 2
+            if by_vector:
+                for s in range(QUAD):
+                    nc.tensor.transpose(
+                        out=dt[:, s, :], in_=dv_last[0][:, s, (b - BLOCKS // 2) * P : (b - BLOCKS // 2 + 1) * P], identity=ident[:]
+                    )
+            for s in range(QUAD if by_vector else PE_PAIRS[g], QUAD):
+                nc.tensor.transpose(out=dt[:, s, :], in_=dv[g][:, s - 1, cols], identity=ident[:])
+            for s in range(first, 0 if by_vector else PE_PAIRS[g]):
                 before = c_of(g - 1, QUAD - 1) if s == 0 else c_of(g, s - 1)
                 nc.tensor.matmul(
                     out=dt[:, s, :], lhsT=before[:, cols], rhs=ident[:],
@@ -254,7 +283,7 @@ def tile_dispatcher_pa_kernel(tc, inv_bytes, inv_scale, Wk, bk, out):
                 func=FUNC.Abs, accum_out=sums[:, b, g : g + 1],
             )
 
-        def st_last_pair():
+        def st_last_pair(q):
             dt = psum.tile([P, BLOCKS, P], F32, name="tp", tag="tp", bufs=4)
             for b in range(BLOCKS):
                 cols = slice(b * P, (b + 1) * P)
@@ -291,7 +320,7 @@ def tile_dispatcher_pa_kernel(tc, inv_bytes, inv_scale, Wk, bk, out):
         stages = {
             "widen": st_widen, "flip": st_flip, "copy": st_copy, "quant": st_quantize, "mult": st_multiply, "bias": st_bias,
             "square": st_square, "clamp": st_clamp, "root": st_root,
-            "factor": st_factor, "c": st_c, "sum": st_sum,
+            "factor": st_factor, "c": st_c, "sum": st_sum, "pairs": st_pairs, "last": st_last_pair, "half": st_half_pairs,
         }
         for i in range(-3, QUADS + 1):
             for step in (FILL_ORDER if i < 0 else ORDER if i < LATE else TURN_ORDER if i == LATE else LATE_ORDER):
@@ -300,7 +329,6 @@ def tile_dispatcher_pa_kernel(tc, inv_bytes, inv_scale, Wk, bk, out):
                         st_weights(0)
                 elif live(i + step[1]):
                     stages[step[0]](i + step[1], *step[2:])
-        st_last_pair()
 
         total = const.tile([P, BLOCKS], F32, name="total")
         nc.vector.tensor_reduce(out=total[:], in_=sums[:], axis=mybir.AxisListType.X, op=ALU.add)

import math
from contextlib import ExitStack

import concourse.mybir as mybir
from concourse.masks import make_identity

F32 = mybir.dt.float32
BF16 = mybir.dt.bfloat16
U32 = mybir.dt.uint32
U8 = mybir.dt.uint8
FP8 = mybir.dt.float8_e4m3fn
FP8X4 = mybir.dt.float8_e4m3fn_x4
ALU = mybir.AluOpType
FUNC = mybir.ActivationFunctionType

P = 128
ROWS = 8192
D = 512
QUAD = 4
HALF = 2
QUADS = ROWS // (P * QUAD)
BLOCKS = D // P
EPS = 1e-8
CLAMP = EPS / math.sqrt(D)

PE_PAIRS = (4, 4, 4, 4, 4, 4, 4, 4, 4, 4, 4, 3, 3, 3, 4, 4)
NEGATED = (0, 2)
SCALAR_C = (1,)
LATE = 14
LATE_SQUARES = (3,)

ORDER = (
    ("bias", 0, 0), ("square", 0, 0), ("sum", -2, 0), ("bias", 0, 1), ("square", 0, 1), ("sum", -2, 1),
    ("bias", 0, 2), ("square", 0, 2), ("bias", 0, 3), ("factor", -1), ("c", -1, 1), ("sum", -2, 2), ("square", 0, 3), ("root", 0),
    ("quant", 1), ("mult", 1), ("sum", -2, 3),
    ("widen", 3, 0), ("widen", 3, 1), ("flip", 3, 0), ("flip", 3, 1),
    ("c", -1, 2), ("c", -1, 3), ("c", -1, 0), ("clamp", 0), ("pairs", -1), ("copy", 3, 0), ("copy", 3, 1),
)
FILL_ORDER = (
    ("quant", 1), ("mult", 1), ("widen", 3, 0), ("flip", 3, 0), ("copy", 3, 0), ("widen", 3, 1), ("flip", 3, 1), ("copy", 3, 1), ("wq", -3),
)
TURN_ORDER = (
    ("bias", 0, 0), ("square", 0, 0),  ("sum", -2, 0), ("bias", 0, 1), ("square", 0, 1), ("sum", -2, 1),
    ("bias", 0, 2), ("square", 0, 2), ("sum", -2, 2), ("bias", 0, 3), ("square", 0, 3), ("root", 0),
    ("factor", -1), ("quant", 1), ("mult", 1), ("c", -1, 1), ("sum", -2, 3),
    ("c", -1, 2), ("c", -1, 3), ("c", -1, 0), ("pairs", -1), ("clamp", 0),
    ("factor", 0), ("c", 0, 1), ("c", 0, 2), ("c", 0, 3), ("c", 0, 0), ("pairs", 0),
    ("sum", -1, 0), ("sum", -1, 1), ("sum", -1, 2), ("sum", -1, 3),
)
LATE_ORDER = (
    ("bias", 0, 0), ("square", 0, 0), ("bias", 0, 1), ("square", 0, 1),
    ("bias", 0, 2), ("square", 0, 2), ("bias", 0, 3), ("square", 0, 3), ("root", 0), ("clamp", 0),
    ("sum", -1, 0), ("sum", -1, 1), ("sum", -1, 2), ("sum", -1, 3),
    ("factor", 0), ("c", 0, 3), ("last", 0), ("c", 0, 2), ("c", 0, 1), ("c", 0, 0), ("half", 0),
)

FLOPS = 2 * ROWS * D * D


def tile_dispatcher_pa_kernel(tc, inv_bytes, inv_scale, Wk, bk, out):
    nc = tc.nc

    with ExitStack() as ctx:
        const = ctx.enter_context(tc.tile_pool(name="const", bufs=1))
        raw = ctx.enter_context(tc.tile_pool(name="raw", bufs=1))
        work = ctx.enter_context(tc.tile_pool(name="work", bufs=2))
        small = ctx.enter_context(tc.tile_pool(name="small", bufs=4))
        psum = ctx.enter_context(tc.psum_pool(name="psum", bufs=2))
        ctx.enter_context(tc.manual_schedule())

        scale_rep = const.tile([P, HALF, D], F32, name="scale_rep")
        nc.scalar.dma_start(
            out=scale_rep[:, 0, :],
            in_=inv_scale.rearrange("a b k -> (a b k)").partition_broadcast(P),
        )
        w_rows = const.tile([P, BLOCKS * D], BF16, name="w_rows")
        bias_rep = const.tile([P, D], BF16, name="bias_rep")

        bytes_view = inv_bytes.rearrange("b t k -> (b t) k").rearrange(
            "(p j) k -> p (j k)", p=P
        )
        byte_tiles = {}
        for q in range(QUADS):
            byte_tiles[q] = raw.tile([P, QUAD * D], U8, name="inv_bytes_%d" % q)
            nc.sync.dma_start(
                out=byte_tiles[q][:],
                in_=bytes_view[:, q * QUAD * D : (q + 1) * QUAD * D],
            )
            if q == 0:
                nc.sync.dma_start(
                    out=w_rows[:].rearrange("n (a k) -> n a k", a=BLOCKS),
                    in_=Wk.rearrange("(a n) k -> n a k", n=P),
                )
            if q == 2:
                nc.sync.dma_start(out=bias_rep[:], in_=bk.partition_broadcast(P))

        one = const.tile([P, 1], F32, name="one")
        nc.vector.memset(one[:], 1.0)
        warm = const.tile([P, 1], F32, name="warm")
        nc.scalar.activation(out=warm[:], in_=one[:], func=FUNC.Abs_reciprocal_sqrt)

        ident = const.tile([P, P], F32, name="ident")
        make_identity(nc, ident[:])
        rotate = const.tile([P, P], F32, name="rotate")
        nc.vector.tensor_copy(out=rotate[:, 0 : P - 1], in_=ident[:, 1:P])
        nc.vector.tensor_copy(out=rotate[:, P - 1 : P], in_=ident[:, 0:1])
        nc.vector.tensor_copy(out=scale_rep[:, 1, :], in_=scale_rep[:, 0, :])

        sums = const.tile([P, BLOCKS, QUADS + 1], F32, name="sums")

        wide, flipped, grouped, codes, planes = {}, {}, {}, {}, {}
        banks, outs, clamped, cs, dv, dv_last = {}, {}, {}, {}, {}, {}
        row_sum, row_sq, inv_norm, factor = {}, {}, {}, {}

        def flip_half(src, h):
            sw = src[:].bitcast(F32).rearrange("p (a m u) -> p a m u", a=QUAD, u=2)
            xt = psum.tile([P, 2, 2, P], F32, name="tp", tag="tp", bufs=4)
            for a in range(2):
                for u in range(2):
                    nc.tensor.transpose(
                        out=xt[:, a, u, :], in_=sw[:, 2 * h + a, :, u], identity=ident[:]
                    )
            return xt

        def copy_half(xt, dst, h):
            dw = dst[:].bitcast(F32).rearrange("p (a r u) -> p a r u", a=QUAD, u=2)
            nc.scalar.copy(
                out=dw[:, 2 * h : 2 * h + 2, :, :],
                in_=xt[:].rearrange("p a u r -> p a r u"),
            )

        def turn_half(src, dst, h):
            copy_half(flip_half(src, h), dst, h)

        def st_widen(q, h):
            if h == 0:
                wide[q] = work.tile([P, QUAD * D], BF16, name="wide", tag="wide", align_bytes=64)
            cols = slice(h * HALF * D, (h + 1) * HALF * D)
            nc.vector.tensor_tensor(
                out=wide[q][:, cols],
                in0=byte_tiles[q][:, cols].bitcast(FP8),
                in1=scale_rep[:].rearrange("p a k -> p (a k)"),
                op=ALU.mult,
            )

        def st_flip(q, h):
            flipped[(q, h)] = flip_half(wide[q], h)

        def st_copy(q, h):
            if h == 0:
                grouped[q] = work.tile([P, QUAD * D], BF16, name="grouped", tag="grouped", bufs=3, align_bytes=64)
            copy_half(flipped[(q, h)], grouped[q], h)

        def st_quantize(q):
            codes[q] = work.tile([P, QUAD * P], U32, name="x_codes", tag="x_codes", align_bytes=64)
            planes[q] = work.tile([P, QUAD * P], U8, name="x_planes", tag="x_planes", align_bytes=64)
            nc.vector.quantize_mx(
                out=codes[q][:].bitcast(FP8X4), scales=planes[q][:], in_=grouped[q][:]
            )

        def st_multiply(q):
            for a in range(QUAD):
                banks[(q, a)] = psum.tile([P, D], F32, name="mx", tag="mx", bufs=4)
                nc.tensor.matmul_mx(
                    out=banks[(q, a)][:],
                    lhsT=codes[q][:, a * P : (a + 1) * P].bitcast(FP8X4),
                    lhsT_scale=planes[q][:, a * P : (a + 1) * P],
                    rhs=w_codes[:].bitcast(FP8X4),
                    rhs_scale=w_planes[:],
                    start=True,
                    stop=True,
                )

        def st_bias(q, a):
            if a == 0:
                outs[q] = work.tile([P, QUAD, D], F32, name="outs", tag="outs")
                row_sum[q] = small.tile([P, QUAD], F32, name="row_sum", tag="row_sum")
            nc.vector.scalar_tensor_tensor(
                out=outs[q][:, a, :], in0=banks[(q, a)][:], scalar=1.0, in1=bias_rep[:],
                op0=ALU.mult, op1=ALU.add, accum_out=row_sum[q][:, a : a + 1],
            )

        def st_square(q, a):
            if a == 0:
                row_sq[q] = small.tile([P, QUAD], F32, name="row_sq", tag="row_sq")
            if q >= LATE and a in LATE_SQUARES:
                junk_v = work.tile([P, D], BF16, name="junk_v", tag="junk_v")
                nc.vector.scalar_tensor_tensor(
                    out=junk_v[:], in0=outs[q][:, a, :], scalar=1.0, in1=outs[q][:, a, :],
                    op0=ALU.mult, op1=ALU.mult, accum_out=row_sq[q][:, a : a + 1],
                )
                return
            junk = work.tile([P, D], BF16, name="junk", tag="junk")
            nc.scalar.activation(
                out=junk[:], in_=outs[q][:, a, :], func=FUNC.Square,
                accum_out=row_sq[q][:, a : a + 1],
            )

        def st_clamp(q):
            clamped[q] = work.tile([P, QUAD, D], F32, name="clamped", tag="clamped", bufs=1)
            engine = nc.gpsimd if q < LATE else nc.vector
            engine.tensor_scalar(
                out=clamped[q][:], in0=outs[q][:], scalar1=CLAMP, scalar2=-CLAMP,
                op0=ALU.min, op1=ALU.max,
            )

        def st_root(q):
            inv_norm[q] = small.tile([P, QUAD], F32, name="inv_norm", tag="inv_norm")
            nc.scalar.activation(
                out=inv_norm[q][:], in_=row_sq[q][:], func=FUNC.Abs_reciprocal_sqrt, scale=EPS * EPS
            )

        def st_factor(q):
            factor[q] = small.tile([P, QUAD], F32, name="factor", tag="factor")
            nc.vector.scalar_tensor_tensor(
                out=factor[q][:], in0=inv_norm[q][:], scalar=1.0 / (EPS * EPS), in1=row_sum[q][:],
                op0=ALU.min, op1=ALU.mult,
            )
            cs[q] = work.tile([P, QUAD, D], F32, name="cs", tag="cs", bufs=3)

        def c_of(q, a):
            return c_first[:] if (q == 0 and a == 0) else cs[q][:, a, :]

        def st_c(q, a):
            if a in SCALAR_C and q < LATE - 1:
                nc.scalar.activation(
                    out=c_of(q, a), in_=clamped[q][:, a, :], func=FUNC.Copy,
                    scale=factor[q][:, a : a + 1],
                )
            else:
                nc.vector.tensor_scalar(
                    out=c_of(q, a), in0=clamped[q][:, a, :], scalar1=factor[q][:, a : a + 1],
                    scalar2=(-1.0 if a in NEGATED else 1.0), op0=ALU.mult, op1=ALU.mult,
                )

        def st_pairs(q):
            lo = PE_PAIRS[q]
            if lo < QUAD:
                dv[q] = work.tile([P, QUAD - 1, D], F32, name="dv", tag="dv")
                nc.vector.tensor_tensor(
                    out=dv[q][:, lo - 1 : QUAD - 1, :], in0=cs[q][:, lo:QUAD, :], in1=cs[q][:, lo - 1 : QUAD - 1, :], op=ALU.add,
                )

        def st_half_pairs(q):
            half = slice(D // 2, D)
            dv_last[0] = work.tile([P, QUAD, D // 2], F32, name="dv_last", tag="dv_last", bufs=1)
            nc.vector.tensor_tensor(
                out=dv_last[0][:, 1:QUAD, :], in0=cs[q][:, 1:QUAD, half], in1=cs[q][:, 0 : QUAD - 1, half], op=ALU.add,
            )
            nc.vector.tensor_tensor(
                out=dv_last[0][:, 0, :], in0=cs[q][:, 0, half], in1=cs[q - 1][:, QUAD - 1, half], op=ALU.add,
            )

        def st_sum(g, b):
            cols = slice(b * P, (b + 1) * P)
            if g == QUADS - 1:
                dt = psum.tile([P, QUAD, P], F32, name="mx", tag="mx", bufs=4)
            else:
                dt = psum.tile([P, QUAD, P], F32, name="tp", tag="tp", bufs=4)
            first = 1 if g == 0 else 0
            by_vector = g == QUADS - 1 and b >= BLOCKS // 2
            if by_vector:
                for s in range(QUAD):
                    nc.tensor.transpose(
                        out=dt[:, s, :], in_=dv_last[0][:, s, (b - BLOCKS // 2) * P : (b - BLOCKS // 2 + 1) * P], identity=ident[:]
                    )
            for s in range(QUAD if by_vector else PE_PAIRS[g], QUAD):
                nc.tensor.transpose(out=dt[:, s, :], in_=dv[g][:, s - 1, cols], identity=ident[:])
            for s in range(first, 0 if by_vector else PE_PAIRS[g]):
                before = c_of(g - 1, QUAD - 1) if s == 0 else c_of(g, s - 1)
                nc.tensor.matmul(
                    out=dt[:, s, :], lhsT=before[:, cols], rhs=ident[:],
                    start=True, stop=False, is_transpose=True,
                )
                nc.tensor.matmul(
                    out=dt[:, s, :], lhsT=c_of(g, s)[:, cols], rhs=ident[:],
                    start=False, stop=True, is_transpose=True,
                )
            junk = work.tile([P, D], BF16, name="junk", tag="junk")
            nc.scalar.activation(
                out=junk[:, first * P : D],
                in_=dt[:].rearrange("p a r -> p (a r)")[:, first * P : D],
                func=FUNC.Abs, accum_out=sums[:, b, g : g + 1],
            )

        def st_last_pair(q):
            dt = psum.tile([P, BLOCKS, P], F32, name="tp", tag="tp", bufs=4)
            for b in range(BLOCKS):
                cols = slice(b * P, (b + 1) * P)
                nc.tensor.matmul(
                    out=dt[:, b, :], lhsT=c_first[:, cols], rhs=rotate[:],
                    start=True, stop=False, is_transpose=True,
                )
                nc.tensor.matmul(
                    out=dt[:, b, :], lhsT=cs[QUADS - 1][:, QUAD - 1, cols], rhs=ident[:],
                    start=False, stop=True, is_transpose=True,
                )
            for b in range(BLOCKS):
                junk = work.tile([P, D], BF16, name="junk", tag="junk")
                nc.scalar.activation(
                    out=junk[:, 0 : P - 1], in_=dt[:, b, 0 : P - 1], func=FUNC.Abs,
                    accum_out=sums[:, b, QUADS : QUADS + 1],
                )

        w_grouped = const.tile([P, BLOCKS * D], BF16, name="w_grouped", align_bytes=64)
        turn_half(w_rows, w_grouped, 0)
        turn_half(w_rows, w_grouped, 1)
        w_codes = const.tile([P, D], U32, name="w_codes", align_bytes=64)
        w_planes = const.tile([P, D], U8, name="w_planes", align_bytes=64)
        c_first = const.tile([P, D], F32, name="c_first")

        def live(q):
            return 0 <= q < QUADS

        def st_weights(q):
            nc.vector.quantize_mx(
                out=w_codes[:].bitcast(FP8X4), scales=w_planes[:], in_=w_grouped[:]
            )

        stages = {
            "widen": st_widen, "flip": st_flip, "copy": st_copy, "quant": st_quantize, "mult": st_multiply, "bias": st_bias,
            "square": st_square, "clamp": st_clamp, "root": st_root,
            "factor": st_factor, "c": st_c, "sum": st_sum, "pairs": st_pairs, "last": st_last_pair, "half": st_half_pairs,
        }
        for i in range(-3, QUADS + 1):
            for step in (FILL_ORDER if i < 0 else ORDER if i < LATE else TURN_ORDER if i == LATE else LATE_ORDER):
                if step[0] == "wq":
                    if i == step[1]:
                        st_weights(0)
                elif live(i + step[1]):
                    stages[step[0]](i + step[1], *step[2:])

        total = const.tile([P, BLOCKS], F32, name="total")
        nc.vector.tensor_reduce(out=total[:], in_=sums[:], axis=mybir.AxisListType.X, op=ALU.add)
        spread = psum.tile([P, D], F32, name="mx", tag="mx", bufs=4)
        for b in range(BLOCKS):
            nc.tensor.transpose(
                out=spread[:, b * P : (b + 1) * P],
                in_=total[:, b : b + 1].to_broadcast([P, P]),
                identity=ident[:],
            )
        result = const.tile([P, D], F32, name="result")
        nc.vector.tensor_copy(out=result[:, 0 : D // 2], in_=spread[:, 0 : D // 2])
        nc.scalar.copy(out=result[:, D // 2 : D], in_=spread[:, D // 2 : D])
        out_view = out.rearrange("(e p) d -> e p d", p=P)
        for e in range(D // P):
            if e % 2 == 0:
                nc.sync.dma_start(out=out_view[e], in_=result[:])
            else:
                nc.scalar.dma_start(out=out_view[e], in_=result[:])
